import numpy as np
import ml_dtypes


def mxq(x, axis, fmt="e4m3"):
    dtype, down = {"e4m3": (ml_dtypes.float8_e4m3fn, 7), "e5m2": (ml_dtypes.float8_e5m2, 14)}[fmt]
    v = np.moveaxis(np.asarray(x, np.float32).astype(ml_dtypes.bfloat16).astype(np.float64), axis, -1)
    blocks = v.reshape(v.shape[:-1] + (-1, 32))
    amax = np.abs(blocks).max(-1, keepdims=True)
    byte = np.maximum(np.where(amax > 0, np.frexp(amax)[1] - 1 + 127, 0) - down, 1)
    scale = np.exp2(byte - 127.0)
    codes = (blocks / scale).astype(np.float32).astype(dtype).astype(np.float64)
    return np.moveaxis((codes * scale).reshape(v.shape), -1, axis)


WIDE = False


def mx_kscale(k):
    if not WIDE:
        return np.ones(k)
    levels = np.array([10, -10, 5, -5, 0])
    a = np.random.permutation(np.resize(levels, k // 512 * 4)).reshape(k // 512, 4)
    idx = np.arange(k)
    return np.exp2(a[idx // 512, idx % 128 // 32])


BF16 = ml_dtypes.bfloat16


def bf(x):
    return np.asarray(x, np.float32).astype(BF16)


def f64(x):
    return np.asarray(x).astype(np.float64)


B, N, D, H, DH = 2, 2048, 512, 4, 64
INNER = H * DH


def dpfp(u):
    u2 = np.concatenate([np.maximum(u, 0.0), np.maximum(-u, 0.0)], axis=-1)
    return u2 * np.roll(u2, 1, axis=-1)


def heads(t):
    return t.reshape(B, N, H, DH).transpose(0, 2, 1, 3)


def setup_inputs():
    s = mx_kscale(D)
    return {"x": bf(np.random.standard_normal((B, N, D)) * s),
            "w_qk": bf(np.random.standard_normal((D, 2 * INNER)) / np.sqrt(D) / s[:, None])}


def reference(x, w_qk):
    qk = mxq(f64(x), 2, "e4m3") @ mxq(f64(w_qk), 0, "e4m3")
    q, k = np.split(qk, 2, axis=-1)
    q, k = dpfp(heads(q)), dpfp(heads(k))
    return q / q.sum(-1, keepdims=True), k / k.sum(-1, keepdims=True)

@@ -1,0 +1,140 @@
+from contextlib import ExitStack
+
+import concourse.bass as bass
+import concourse.mybir as mybir
+import concourse.tile as tile
+from concourse.masks import make_identity
+
+F32 = mybir.dt.float32
+BF16 = mybir.dt.bfloat16
+U32 = mybir.dt.uint32
+U8 = mybir.dt.uint8
+FP8X4 = mybir.dt.float8_e4m3fn_x4
+ALU = mybir.AluOpType
+ACT = mybir.ActivationFunctionType
+
+P = 128
+D = 512
+TOKENS = 4096
+SEQ = 2048
+G = 8
+DH = 64
+T = 4
+BLOCK = P * T
+NB = TOKENS // BLOCK
+PADW = 68
+
+FLOPS = 2 * TOKENS * D * D
+
+
+def tile_dpfpattention_pa_t_kernel(tc, x, w_qk, out_0, out_1):
+    nc = tc.nc
+    x_flat = x.flatten_outer_dims()
+    with ExitStack() as ctx:
+        const = ctx.enter_context(tc.tile_pool(name="const", bufs=1))
+        xin = ctx.enter_context(tc.tile_pool(name="xin", bufs=NB))
+        xq = ctx.enter_context(tc.tile_pool(name="xq", bufs=3))
+        work = ctx.enter_context(tc.tile_pool(name="work", bufs=3))
+        outp = ctx.enter_context(tc.tile_pool(name="outp", bufs=3))
+        ps_t = ctx.enter_context(tc.psum_pool(name="ps_t", bufs=3))
+        ps_a = ctx.enter_context(tc.psum_pool(name="ps_a", bufs=5))
+
+        w_sb = const.tile([P, 4, D], BF16)
+        nc.sync.dma_start(
+            out=w_sb[:].rearrange("q (u e) c -> q u (e c)", u=2),
+            in_=w_qk.rearrange("(u q e) c -> q u (e c)", u=2, e=2),
+        )
+        x_sbs = []
+        for b in range(NB):
+            x_sb = xin.tile([P, T * D], BF16, name="x_sb")
+            nc.sync.dma_start(
+                out=x_sb[:],
+                in_=x_flat[b * BLOCK:(b + 1) * BLOCK, :].rearrange("(p j) k -> p (j k)", j=T),
+            )
+            x_sbs.append(x_sb)
+
+        ident = const.tile([P, P], F32)
+        make_identity(nc, ident[:])
+
+        w_grp = const.tile([P, D * 4], BF16, align_bytes=64)
+        nc.vector.tensor_copy(
+            out=w_grp[:].rearrange("p (c i t) -> p c t i", i=4, t=4),
+            in_=w_sb[:].rearrange("p t (c i) -> p c t i", i=4),
+        )
+        w_codes = const.tile([P, D], U32, align_bytes=64)
+        w_scales = const.tile([P, D], U8, align_bytes=64)
+        nc.vector.quantize_mx(out=w_codes[:].bitcast(FP8X4), scales=w_scales[:], in_=w_grp[:])
+
+        for b in range(NB):
+            xw = x_sbs[b][:].bitcast(F32)
+            x_grp = xq.tile([P, T * D], BF16, align_bytes=64)
+            xg32 = x_grp[:].bitcast(F32)
+            for h in range(T // 2):
+                xt = ps_t.tile([P, 2, 2, P], F32)
+                for jj in range(2):
+                    j = 2 * h + jj
+                    for u in range(2):
+                        c0 = j * 256 + u * P
+                        nc.tensor.transpose(xt[:, jj, u, :], xw[:, c0:c0 + P], ident[:])
+                nc.scalar.copy(
+                    out=xg32[:, h * 512:(h + 1) * 512].rearrange("p (j r u) -> p j r u", j=2, u=2),
+                    in_=xt[:].rearrange("p j u r -> p j r u"),
+                )
+            x_codes = xq.tile([P, T * P], U32, align_bytes=64)
+            x_scales = xq.tile([P, T * P], U8, align_bytes=64)
+            nc.vector.quantize_mx(out=x_codes[:].bitcast(FP8X4), scales=x_scales[:], in_=x_grp[:])
+
+            u_pad = work.tile([P, G * T, PADW], F32)
+            u_view = u_pad[:].rearrange("p (g j) i -> p g j i", j=T)
+            for j in range(T):
+                acc = ps_a.tile([P, D], F32)
+                nc.tensor.matmul_mx(
+                    out=acc[:],
+                    lhsT=x_codes[:, j * P:(j + 1) * P].bitcast(FP8X4),
+                    lhsT_scale=x_scales[:, j * P:(j + 1) * P],
+                    rhs=w_codes[:].bitcast(FP8X4),
+                    rhs_scale=w_scales[:],
+                    start=True,
+                    stop=True,
+                )
+                acc3 = acc[:].rearrange("p (g i) -> p g i", g=G)
+                nc.scalar.copy(out=u_view[:, :, j, 4:PADW], in_=acc3)
+                nc.scalar.activation(
+                    out=u_view[:, :, j, 3:4], in_=acc3[:, :, DH - 1:DH], func=ACT.Copy, scale=-1.0
+                )
+
+            prod = work.tile([P, G * T, DH], F32)
+            nc.vector.tensor_tensor(
+                out=prod[:], in0=u_pad[:, :, 4:PADW], in1=u_pad[:, :, 3:PADW - 1], op=ALU.mult
+            )
+            rp = work.tile([P, G * T, DH], F32)
+            ssum = work.tile([P, G * T], F32)
+            for gj in range(G * T):
+                nc.scalar.activation(
+                    out=rp[:, gj, :], in_=prod[:, gj, :], func=ACT.Relu,
+                    accum_out=ssum[:, gj:gj + 1],
+                )
+            rinv = work.tile([P, G * T], F32)
+            nc.vector.reciprocal(rinv[:], ssum[:])
+            nrm = work.tile([P, G * T, DH], F32)
+            nc.vector.tensor_tensor(
+                out=nrm[:], in0=rp[:], in1=rinv[:].unsqueeze(2).to_broadcast([P, G * T, DH]),
+                op=ALU.mult,
+            )
+            o_sb = outp.tile([P, G * T, 2 * DH], F32)
+            nc.vector.scalar_tensor_tensor(
+                out=o_sb[:, :, 0:DH], in0=u_pad[:, :, 4:PADW], scalar=0.0, in1=nrm[:],
+                op0=ALU.is_gt, op1=ALU.mult,
+            )
+            nc.vector.scalar_tensor_tensor(
+                out=o_sb[:, :, DH:2 * DH], in0=u_pad[:, :, 4:PADW], scalar=0.0, in1=nrm[:],
+                op0=ALU.is_lt, op1=ALU.mult,
+            )
+            bb = (b * BLOCK) // SEQ
+            n0 = (b * BLOCK) % SEQ
+            half = (G // 2) * T
+            for dst, lo in ((out_0, 0), (out_1, half)):
+                nc.sync.dma_start(
+                    out=dst[bb, :, n0:n0 + BLOCK, :].rearrange("h (p j) f -> p h (j f)", j=T),
+                    in_=o_sb[:, lo:lo + half, :].rearrange("p (h j) f -> p h (j f)", j=T),
+                )

@@ -1,8 +1,6 @@
 from contextlib import ExitStack
 
-import concourse.bass as bass
 import concourse.mybir as mybir
-import concourse.tile as tile
 from concourse.masks import make_identity
 
 F32 = mybir.dt.float32
@@ -17,12 +15,14 @@ P = 128
 D = 512
 TOKENS = 4096
 SEQ = 2048
+NT = TOKENS // P
 G = 8
 DH = 64
-T = 4
-BLOCK = P * T
-NB = TOKENS // BLOCK
 PADW = 68
+BLOCK_T = (4, 4, 4, 4, 4, 4, 4, 2, 1, 1)
+QUANT_TILES = (4, 4, 8, 8, 8)
+NEG_ON_G = (2, 5, 8, 11, 14, 17, 20, 23, 26)
+M_ON_V = (30, 31)
 
 FLOPS = 2 * TOKENS * D * D
 
@@ -30,14 +30,29 @@ FLOPS = 2 * TOKENS * D * D
 def tile_dpfpattention_pa_t_kernel(tc, x, w_qk, out_0, out_1):
     nc = tc.nc
     x_flat = x.flatten_outer_dims()
+    tile_block = []
+    tile_j = []
+    block_tile0 = []
+    for b, t_b in enumerate(BLOCK_T):
+        block_tile0.append(len(tile_block))
+        for j in range(t_b):
+            tile_block.append(b)
+            tile_j.append(j)
+    assert len(tile_block) == NT
+    q_start = [sum(QUANT_TILES[:q]) for q in range(len(QUANT_TILES))]
+    assert sum(QUANT_TILES) == NT
+    tile_q = []
+    for q, n_q in enumerate(QUANT_TILES):
+        tile_q.extend([q] * n_q)
+
     with ExitStack() as ctx:
         const = ctx.enter_context(tc.tile_pool(name="const", bufs=1))
-        xin = ctx.enter_context(tc.tile_pool(name="xin", bufs=NB))
-        xq = ctx.enter_context(tc.tile_pool(name="xq", bufs=3))
-        work = ctx.enter_context(tc.tile_pool(name="work", bufs=3))
+        xq = ctx.enter_context(tc.tile_pool(name="xq", bufs=2))
+        work = ctx.enter_context(tc.tile_pool(name="work", bufs=4))
+        small = ctx.enter_context(tc.tile_pool(name="small", bufs=8))
         outp = ctx.enter_context(tc.tile_pool(name="outp", bufs=3))
-        ps_t = ctx.enter_context(tc.psum_pool(name="ps_t", bufs=3))
-        ps_a = ctx.enter_context(tc.psum_pool(name="ps_a", bufs=5))
+        ps_t = ctx.enter_context(tc.psum_pool(name="ps_t", bufs=2))
+        ps_a = ctx.enter_context(tc.psum_pool(name="ps_a", bufs=6))
 
         w_sb = const.tile([P, 4, D], BF16)
         nc.sync.dma_start(
@@ -45,11 +60,12 @@ def tile_dpfpattention_pa_t_kernel(tc, x, w_qk, out_0, out_1):
             in_=w_qk.rearrange("(u q e) c -> q u (e c)", u=2, e=2),
         )
         x_sbs = []
-        for b in range(NB):
-            x_sb = xin.tile([P, T * D], BF16, name="x_sb")
+        for b, t_b in enumerate(BLOCK_T):
+            x_sb = const.tile([P, t_b * D], BF16, name="x_sb%d" % b)
+            r0 = block_tile0[b] * P
             nc.sync.dma_start(
                 out=x_sb[:],
-                in_=x_flat[b * BLOCK:(b + 1) * BLOCK, :].rearrange("(p j) k -> p (j k)", j=T),
+                in_=x_flat[r0:r0 + t_b * P, :].rearrange("(p j) k -> p (j k)", j=t_b),
             )
             x_sbs.append(x_sb)
 
@@ -65,76 +81,97 @@ def tile_dpfpattention_pa_t_kernel(tc, x, w_qk, out_0, out_1):
         w_scales = const.tile([P, D], U8, align_bytes=64)
         nc.vector.quantize_mx(out=w_codes[:].bitcast(FP8X4), scales=w_scales[:], in_=w_grp[:])
 
-        for b in range(NB):
-            xw = x_sbs[b][:].bitcast(F32)
-            x_grp = xq.tile([P, T * D], BF16, align_bytes=64)
+        codes = {}
+
+        def prep(q):
+            n_q = QUANT_TILES[q]
+            x_grp = xq.tile([P, n_q * D], BF16, align_bytes=64, name="x_grp")
             xg32 = x_grp[:].bitcast(F32)
-            for h in range(T // 2):
-                xt = ps_t.tile([P, 2, 2, P], F32)
+            for h in range(n_q // 2):
+                xt = ps_t.tile([P, 2, 2, P], F32, name="xt")
                 for jj in range(2):
-                    j = 2 * h + jj
+                    i = q_start[q] + 2 * h + jj
+                    xw = x_sbs[tile_block[i]][:].bitcast(F32)
                     for u in range(2):
-                        c0 = j * 256 + u * P
+                        c0 = tile_j[i] * 256 + u * P
                         nc.tensor.transpose(xt[:, jj, u, :], xw[:, c0:c0 + P], ident[:])
                 nc.scalar.copy(
                     out=xg32[:, h * 512:(h + 1) * 512].rearrange("p (j r u) -> p j r u", j=2, u=2),
                     in_=xt[:].rearrange("p j u r -> p j r u"),
                 )
-            x_codes = xq.tile([P, T * P], U32, align_bytes=64)
-            x_scales = xq.tile([P, T * P], U8, align_bytes=64)
+            x_codes = const.tile([P, n_q * P], U32, align_bytes=64, name="x_codes%d" % q)
+            x_scales = const.tile([P, n_q * P], U8, align_bytes=64, name="x_scales%d" % q)
             nc.vector.quantize_mx(out=x_codes[:].bitcast(FP8X4), scales=x_scales[:], in_=x_grp[:])
+            codes[q] = (x_codes, x_scales)
 
-            u_pad = work.tile([P, G * T, PADW], F32)
-            u_view = u_pad[:].rearrange("p (g j) i -> p g j i", j=T)
-            for j in range(T):
-                acc = ps_a.tile([P, D], F32)
-                nc.tensor.matmul_mx(
-                    out=acc[:],
-                    lhsT=x_codes[:, j * P:(j + 1) * P].bitcast(FP8X4),
-                    lhsT_scale=x_scales[:, j * P:(j + 1) * P],
-                    rhs=w_codes[:].bitcast(FP8X4),
-                    rhs_scale=w_scales[:],
-                    start=True,
-                    stop=True,
-                )
-                acc3 = acc[:].rearrange("p (g i) -> p g i", g=G)
-                nc.scalar.copy(out=u_view[:, :, j, 4:PADW], in_=acc3)
-                nc.scalar.activation(
-                    out=u_view[:, :, j, 3:4], in_=acc3[:, :, DH - 1:DH], func=ACT.Copy, scale=-1.0
-                )
-
-            prod = work.tile([P, G * T, DH], F32)
-            nc.vector.tensor_tensor(
-                out=prod[:], in0=u_pad[:, :, 4:PADW], in1=u_pad[:, :, 3:PADW - 1], op=ALU.mult
+        prep(0)
+        prep(1)
+        o_tiles = {}
+        for i in range(NT):
+            q = tile_q[i]
+            if i == q_start[q] and q >= 1 and q + 1 < len(QUANT_TILES):
+                prep(q + 1)
+            b = tile_block[i]
+            j = tile_j[i]
+            t_b = BLOCK_T[b]
+            x_codes, x_scales = codes[q]
+            c0 = (i - q_start[q]) * P
+            acc = ps_a.tile([P, D], F32, name="acc")
+            nc.tensor.matmul_mx(
+                out=acc[:],
+                lhsT=x_codes[:, c0:c0 + P].bitcast(FP8X4),
+                lhsT_scale=x_scales[:, c0:c0 + P],
+                rhs=w_codes[:].bitcast(FP8X4),
+                rhs_scale=w_scales[:],
+                start=True,
+                stop=True,
             )
-            rp = work.tile([P, G * T, DH], F32)
-            ssum = work.tile([P, G * T], F32)
-            for gj in range(G * T):
+            acc3 = acc[:].rearrange("p (g i) -> p g i", g=G)
+            u_pad = work.tile([P, G, PADW], F32, name="u_pad")
+            nc.scalar.copy(out=u_pad[:, :, 4:PADW], in_=acc3)
+            nc.scalar.activation(
+                out=u_pad[:, :, 3:4], in_=acc3[:, :, DH - 1:DH], func=ACT.Copy, scale=-1.0
+            )
+            prod = work.tile([P, G, DH], F32, name="prod")
+            nc.vector.tensor_tensor(out=prod[:], in0=acc3, in1=u_pad[:, :, 3:PADW - 1], op=ALU.mult)
+            rp = work.tile([P, G, DH], F32, name="rp")
+            ssum = small.tile([P, G], F32, name="ssum")
+            for g in range(G):
                 nc.scalar.activation(
-                    out=rp[:, gj, :], in_=prod[:, gj, :], func=ACT.Relu,
-                    accum_out=ssum[:, gj:gj + 1],
+                    out=rp[:, g, :], in_=prod[:, g, :], func=ACT.Relu, accum_out=ssum[:, g:g + 1]
                 )
-            rinv = work.tile([P, G * T], F32)
+            rinv = small.tile([P, G], F32, name="rinv")
             nc.vector.reciprocal(rinv[:], ssum[:])
-            nrm = work.tile([P, G * T, DH], F32)
-            nc.vector.tensor_tensor(
-                out=nrm[:], in0=rp[:], in1=rinv[:].unsqueeze(2).to_broadcast([P, G * T, DH]),
-                op=ALU.mult,
+            nrm = work.tile([P, G, DH], F32, name="nrm")
+            m_eng = nc.vector if i in M_ON_V else nc.gpsimd
+            m_eng.tensor_tensor(
+                out=nrm[:], in0=rp[:], in1=rinv[:].unsqueeze(2).to_broadcast([P, G, DH]), op=ALU.mult
             )
-            o_sb = outp.tile([P, G * T, 2 * DH], F32)
+            if j == 0:
+                o_tiles[b] = outp.tile([P, G * t_b, 2 * DH], F32, name="o_sb")
+            o_sb = o_tiles[b]
+            o_view = o_sb[:].rearrange("p (g j) f -> p g j f", j=t_b)
             nc.vector.scalar_tensor_tensor(
-                out=o_sb[:, :, 0:DH], in0=u_pad[:, :, 4:PADW], scalar=0.0, in1=nrm[:],
+                out=o_view[:, :, j, 0:DH], in0=acc3, scalar=0.0, in1=nrm[:],
                 op0=ALU.is_gt, op1=ALU.mult,
             )
-            nc.vector.scalar_tensor_tensor(
-                out=o_sb[:, :, DH:2 * DH], in0=u_pad[:, :, 4:PADW], scalar=0.0, in1=nrm[:],
-                op0=ALU.is_lt, op1=ALU.mult,
-            )
-            bb = (b * BLOCK) // SEQ
-            n0 = (b * BLOCK) % SEQ
-            half = (G // 2) * T
-            for dst, lo in ((out_0, 0), (out_1, half)):
-                nc.sync.dma_start(
-                    out=dst[bb, :, n0:n0 + BLOCK, :].rearrange("h (p j) f -> p h (j f)", j=T),
-                    in_=o_sb[:, lo:lo + half, :].rearrange("p (h j) f -> p h (j f)", j=T),
+            if i in NEG_ON_G:
+                nc.gpsimd.tensor_tensor(
+                    out=o_view[:, :, j, DH:2 * DH], in0=nrm[:], in1=o_view[:, :, j, 0:DH],
+                    op=ALU.subtract,
                 )
+            else:
+                nc.vector.scalar_tensor_tensor(
+                    out=o_view[:, :, j, DH:2 * DH], in0=acc3, scalar=0.0, in1=nrm[:],
+                    op0=ALU.is_lt, op1=ALU.mult,
+                )
+            if j == t_b - 1:
+                tok0 = block_tile0[b] * P
+                bb = tok0 // SEQ
+                n0 = tok0 % SEQ
+                half = (G // 2) * t_b
+                for dst, lo in ((out_0, 0), (out_1, half)):
+                    nc.sync.dma_start(
+                        out=dst[bb, :, n0:n0 + t_b * P, :].rearrange("h (p j) f -> p h (j f)", j=t_b),
+                        in_=o_sb[:, lo:lo + half, :].rearrange("p (h j) f -> p h (j f)", j=t_b),
+                    )

@@ -19,10 +19,14 @@ NT = TOKENS // P
 G = 8
 DH = 64
 PADW = 68
-BLOCK_T = (4, 4, 4, 4, 4, 4, 4, 2, 1, 1)
-QUANT_TILES = (4, 4, 8, 8, 8)
-NEG_ON_G = (2, 5, 8, 11, 14, 17, 20, 23, 26)
+BLOCK_T = (2, 2, 4, 4, 4, 4, 4, 2, 2, 2, 1, 1)
+QUANT_TILES = (2, 2, 4, 8, 8, 8)
+COPY_STEP = (-1, -1, 0, 0, 1, 2, 3, 4, 6, 8, 10, 12, 14, 16, 18, 20)
+QUANT_STEP = (-1, -1, 2, 6, 14, 22)
+XT_ON_V = (1, 2, 3, 4, 5)
+NEG_ON_G = ()
 M_ON_V = (30, 31)
+OUT_LAG = 3
 
 FLOPS = 2 * TOKENS * D * D
 
@@ -50,9 +54,10 @@ def tile_dpfpattention_pa_t_kernel(tc, x, w_qk, out_0, out_1):
         xq = ctx.enter_context(tc.tile_pool(name="xq", bufs=2))
         work = ctx.enter_context(tc.tile_pool(name="work", bufs=4))
         small = ctx.enter_context(tc.tile_pool(name="small", bufs=8))
-        outp = ctx.enter_context(tc.tile_pool(name="outp", bufs=3))
+        outp = ctx.enter_context(tc.tile_pool(name="outp", bufs=5))
         ps_t = ctx.enter_context(tc.psum_pool(name="ps_t", bufs=2))
         ps_a = ctx.enter_context(tc.psum_pool(name="ps_a", bufs=6))
+        ctx.enter_context(tc.manual_schedule())
 
         w_sb = const.tile([P, 4, D], BF16)
         nc.sync.dma_start(
@@ -81,39 +86,50 @@ def tile_dpfpattention_pa_t_kernel(tc, x, w_qk, out_0, out_1):
         w_scales = const.tile([P, D], U8, align_bytes=64)
         nc.vector.quantize_mx(out=w_codes[:].bitcast(FP8X4), scales=w_scales[:], in_=w_grp[:])
 
+        xts = {}
+        x_grps = {}
         codes = {}
+        accs = {}
+        u_pads = {}
+        prods = {}
+        rps = {}
+        ssums = {}
+        nrms = {}
+        o_tiles = {}
 
-        def prep(q):
+        def transposes(k):
+            xt = ps_t.tile([P, 2, 2, P], F32, name="xt")
+            for jj in range(2):
+                i = 2 * k + jj
+                xw = x_sbs[tile_block[i]][:].bitcast(F32)
+                for u in range(2):
+                    c0 = tile_j[i] * 256 + u * P
+                    nc.tensor.transpose(xt[:, jj, u, :], xw[:, c0:c0 + P], ident[:])
+            xts[k] = xt
+
+        def copy_out(k):
+            q = tile_q[2 * k]
+            if 2 * k == q_start[q]:
+                x_grps[q] = xq.tile([P, QUANT_TILES[q] * D], BF16, align_bytes=64, name="x_grp")
+            h = k - q_start[q] // 2
+            dst = x_grps[q][:].bitcast(F32)[:, h * 512:(h + 1) * 512].rearrange(
+                "p (j r u) -> p j r u", j=2, u=2)
+            src = xts[k][:].rearrange("p j u r -> p j r u")
+            if k in XT_ON_V:
+                nc.vector.tensor_copy(out=dst, in_=src)
+            else:
+                nc.scalar.copy(out=dst, in_=src)
+
+        def quantise(q):
             n_q = QUANT_TILES[q]
-            x_grp = xq.tile([P, n_q * D], BF16, align_bytes=64, name="x_grp")
-            xg32 = x_grp[:].bitcast(F32)
-            for h in range(n_q // 2):
-                xt = ps_t.tile([P, 2, 2, P], F32, name="xt")
-                for jj in range(2):
-                    i = q_start[q] + 2 * h + jj
-                    xw = x_sbs[tile_block[i]][:].bitcast(F32)
-                    for u in range(2):
-                        c0 = tile_j[i] * 256 + u * P
-                        nc.tensor.transpose(xt[:, jj, u, :], xw[:, c0:c0 + P], ident[:])
-                nc.scalar.copy(
-                    out=xg32[:, h * 512:(h + 1) * 512].rearrange("p (j r u) -> p j r u", j=2, u=2),
-                    in_=xt[:].rearrange("p j u r -> p j r u"),
-                )
             x_codes = const.tile([P, n_q * P], U32, align_bytes=64, name="x_codes%d" % q)
             x_scales = const.tile([P, n_q * P], U8, align_bytes=64, name="x_scales%d" % q)
-            nc.vector.quantize_mx(out=x_codes[:].bitcast(FP8X4), scales=x_scales[:], in_=x_grp[:])
+            nc.vector.quantize_mx(
+                out=x_codes[:].bitcast(FP8X4), scales=x_scales[:], in_=x_grps[q][:])
             codes[q] = (x_codes, x_scales)
 
-        prep(0)
-        prep(1)
-        o_tiles = {}
-        for i in range(NT):
+        def project(i):
             q = tile_q[i]
-            if i == q_start[q] and q >= 1 and q + 1 < len(QUANT_TILES):
-                prep(q + 1)
-            b = tile_block[i]
-            j = tile_j[i]
-            t_b = BLOCK_T[b]
             x_codes, x_scales = codes[q]
             c0 = (i - q_start[q]) * P
             acc = ps_a.tile([P, D], F32, name="acc")
@@ -126,52 +142,103 @@ def tile_dpfpattention_pa_t_kernel(tc, x, w_qk, out_0, out_1):
                 start=True,
                 stop=True,
             )
-            acc3 = acc[:].rearrange("p (g i) -> p g i", g=G)
+            accs[i] = acc[:].rearrange("p (g i) -> p g i", g=G)
+
+        def stage_up(i):
             u_pad = work.tile([P, G, PADW], F32, name="u_pad")
-            nc.scalar.copy(out=u_pad[:, :, 4:PADW], in_=acc3)
+            nc.scalar.copy(out=u_pad[:, :, 4:PADW], in_=accs[i])
             nc.scalar.activation(
-                out=u_pad[:, :, 3:4], in_=acc3[:, :, DH - 1:DH], func=ACT.Copy, scale=-1.0
-            )
+                out=u_pad[:, :, 3:4], in_=accs[i][:, :, DH - 1:DH], func=ACT.Copy, scale=-1.0)
+            u_pads[i] = u_pad
+
+        def stage_p(i):
             prod = work.tile([P, G, DH], F32, name="prod")
-            nc.vector.tensor_tensor(out=prod[:], in0=acc3, in1=u_pad[:, :, 3:PADW - 1], op=ALU.mult)
+            nc.vector.tensor_tensor(
+                out=prod[:], in0=accs[i], in1=u_pads[i][:, :, 3:PADW - 1], op=ALU.mult)
+            prods[i] = prod
+
+        def stage_sum(i):
             rp = work.tile([P, G, DH], F32, name="rp")
             ssum = small.tile([P, G], F32, name="ssum")
             for g in range(G):
                 nc.scalar.activation(
-                    out=rp[:, g, :], in_=prod[:, g, :], func=ACT.Relu, accum_out=ssum[:, g:g + 1]
-                )
+                    out=rp[:, g, :], in_=prods[i][:, g, :], func=ACT.Relu,
+                    accum_out=ssum[:, g:g + 1])
+            rps[i] = rp
+            ssums[i] = ssum
+
+        def stage_norm(i):
             rinv = small.tile([P, G], F32, name="rinv")
-            nc.vector.reciprocal(rinv[:], ssum[:])
+            nc.vector.reciprocal(rinv[:], ssums[i][:])
             nrm = work.tile([P, G, DH], F32, name="nrm")
             m_eng = nc.vector if i in M_ON_V else nc.gpsimd
             m_eng.tensor_tensor(
-                out=nrm[:], in0=rp[:], in1=rinv[:].unsqueeze(2).to_broadcast([P, G, DH]), op=ALU.mult
-            )
+                out=nrm[:], in0=rps[i][:], in1=rinv[:].unsqueeze(2).to_broadcast([P, G, DH]),
+                op=ALU.mult)
+            nrms[i] = nrm
+
+        def stage_out(i):
+            b = tile_block[i]
+            j = tile_j[i]
+            t_b = BLOCK_T[b]
             if j == 0:
                 o_tiles[b] = outp.tile([P, G * t_b, 2 * DH], F32, name="o_sb")
             o_sb = o_tiles[b]
             o_view = o_sb[:].rearrange("p (g j) f -> p g j f", j=t_b)
             nc.vector.scalar_tensor_tensor(
-                out=o_view[:, :, j, 0:DH], in0=acc3, scalar=0.0, in1=nrm[:],
-                op0=ALU.is_gt, op1=ALU.mult,
-            )
+                out=o_view[:, :, j, 0:DH], in0=accs[i], scalar=0.0, in1=nrms[i][:],
+                op0=ALU.is_gt, op1=ALU.mult)
             if i in NEG_ON_G:
                 nc.gpsimd.tensor_tensor(
-                    out=o_view[:, :, j, DH:2 * DH], in0=nrm[:], in1=o_view[:, :, j, 0:DH],
-                    op=ALU.subtract,
-                )
+                    out=o_view[:, :, j, DH:2 * DH], in0=nrms[i][:], in1=o_view[:, :, j, 0:DH],
+                    op=ALU.subtract)
             else:
                 nc.vector.scalar_tensor_tensor(
-                    out=o_view[:, :, j, DH:2 * DH], in0=acc3, scalar=0.0, in1=nrm[:],
-                    op0=ALU.is_lt, op1=ALU.mult,
+                    out=o_view[:, :, j, DH:2 * DH], in0=accs[i], scalar=0.0, in1=nrms[i][:],
+                    op0=ALU.is_lt, op1=ALU.mult)
+
+        def store(b):
+            t_b = BLOCK_T[b]
+            tok0 = block_tile0[b] * P
+            bb = tok0 // SEQ
+            n0 = tok0 % SEQ
+            half = (G // 2) * t_b
+            for dst, lo in ((out_0, 0), (out_1, half)):
+                nc.sync.dma_start(
+                    out=dst[bb, :, n0:n0 + t_b * P, :].rearrange("h (p j) f -> p h (j f)", j=t_b),
+                    in_=o_tiles[b][:, lo:lo + half, :].rearrange("p (h j) f -> p h (j f)", j=t_b),
                 )
-            if j == t_b - 1:
-                tok0 = block_tile0[b] * P
-                bb = tok0 // SEQ
-                n0 = tok0 % SEQ
-                half = (G // 2) * t_b
-                for dst, lo in ((out_0, 0), (out_1, half)):
-                    nc.sync.dma_start(
-                        out=dst[bb, :, n0:n0 + t_b * P, :].rearrange("h (p j) f -> p h (j f)", j=t_b),
-                        in_=o_sb[:, lo:lo + half, :].rearrange("p (h j) f -> p h (j f)", j=t_b),
-                    )
+
+        for k in range(NT // 2):
+            if COPY_STEP[k] < 0:
+                transposes(k)
+                copy_out(k)
+        for q in range(len(QUANT_TILES)):
+            if QUANT_STEP[q] < 0:
+                quantise(q)
+        project(0)
+        for n in range(NT + OUT_LAG):
+            for k in range(NT // 2):
+                if COPY_STEP[k] == n:
+                    transposes(k)
+            if n + 1 < NT:
+                project(n + 1)
+            if 0 <= n - 2 < NT:
+                stage_norm(n - 2)
+            if n < NT:
+                stage_up(n)
+            if 0 <= n - OUT_LAG < NT:
+                stage_out(n - OUT_LAG)
+            if 0 <= n - 1 < NT:
+                stage_sum(n - 1)
+            if n < NT:
+                stage_p(n)
+            for k in range(NT // 2):
+                if COPY_STEP[k] == n:
+                    copy_out(k)
+            for q in range(len(QUANT_TILES)):
+                if QUANT_STEP[q] == n:
+                    quantise(q)
+            i = n - OUT_LAG
+            if 0 <= i < NT and tile_j[i] == BLOCK_T[tile_block[i]] - 1:
+                store(tile_block[i])

@@ -18,15 +18,17 @@ SEQ = 2048
 NT = TOKENS // P
 G = 8
 DH = 64
-PADW = 68
-BLOCK_T = (2, 2, 4, 4, 4, 4, 4, 2, 2, 2, 1, 1)
+HK = DH // 2
+OPAD = 36
+BLOCK_T = (2, 2, 4, 4, 4, 4, 2, 2, 2, 2, 2, 1, 1)
 QUANT_TILES = (2, 2, 4, 8, 8, 8)
-COPY_STEP = (-1, -1, 0, 0, 1, 2, 3, 4, 6, 8, 10, 12, 14, 16, 18, 20)
-QUANT_STEP = (-1, -1, 2, 6, 14, 22)
+COPY_STEP = (-1, -1, 0, 1, 2, 3, 4, 5, 6, 8, 10, 12, 14, 16, 18, 20)
+QUANT_STEP = (-1, -1, 1, 5, 13, 21)
 XT_ON_V = (1, 2, 3, 4, 5)
-NEG_ON_G = ()
-M_ON_V = (30, 31)
-OUT_LAG = 3
+NEG_ON_G = (2, 5, 8, 11, 14, 17, 20, 23)
+M_ON_V = ()
+M_ON_S = (30, 31)
+OUT_LAG = 4
 
 FLOPS = 2 * TOKENS * D * D
 
@@ -90,7 +92,7 @@ def tile_dpfpattention_pa_t_kernel(tc, x, w_qk, out_0, out_1):
         x_grps = {}
         codes = {}
         accs = {}
-        u_pads = {}
+        odds = {}
         prods = {}
         rps = {}
         ssums = {}
@@ -142,19 +144,23 @@ def tile_dpfpattention_pa_t_kernel(tc, x, w_qk, out_0, out_1):
                 start=True,
                 stop=True,
             )
-            accs[i] = acc[:].rearrange("p (g i) -> p g i", g=G)
+            accs[i] = acc
 
         def stage_up(i):
-            u_pad = work.tile([P, G, PADW], F32, name="u_pad")
-            nc.scalar.copy(out=u_pad[:, :, 4:PADW], in_=accs[i])
+            acc4 = accs[i][:].rearrange("p (g k e) -> p g k e", g=G, e=2)
+            odd = work.tile([P, G, OPAD], F32, name="odd")
+            nc.scalar.copy(out=odd[:, :, 4:OPAD], in_=acc4[:, :, :, 1])
             nc.scalar.activation(
-                out=u_pad[:, :, 3:4], in_=accs[i][:, :, DH - 1:DH], func=ACT.Copy, scale=-1.0)
-            u_pads[i] = u_pad
+                out=odd[:, :, 3:4], in_=acc4[:, :, HK - 1:HK, 1], func=ACT.Copy, scale=-1.0)
+            odds[i] = odd
 
         def stage_p(i):
-            prod = work.tile([P, G, DH], F32, name="prod")
-            nc.vector.tensor_tensor(
-                out=prod[:], in0=accs[i], in1=u_pads[i][:, :, 3:PADW - 1], op=ALU.mult)
+            even = accs[i][:].rearrange("p (g k e) -> p g k e", g=G, e=2)[:, :, :, 0]
+            prod = work.tile([P, G, 2, HK], F32, name="prod")
+            for e in range(2):
+                nc.vector.tensor_tensor(
+                    out=prod[:, :, e, :], in0=even, in1=odds[i][:, :, 3 + e:3 + e + HK],
+                    op=ALU.mult)
             prods[i] = prod
 
         def stage_sum(i):
@@ -162,8 +168,9 @@ def tile_dpfpattention_pa_t_kernel(tc, x, w_qk, out_0, out_1):
             ssum = small.tile([P, G], F32, name="ssum")
             for g in range(G):
                 nc.scalar.activation(
-                    out=rp[:, g, :], in_=prods[i][:, g, :], func=ACT.Relu,
-                    accum_out=ssum[:, g:g + 1])
+                    out=rp[:, g, :].rearrange("p (k e) -> p k e", e=2),
+                    in_=prods[i][:, g, :, :].rearrange("p e k -> p k e"),
+                    func=ACT.Relu, accum_out=ssum[:, g:g + 1])
             rps[i] = rp
             ssums[i] = ssum
 
@@ -171,11 +178,30 @@ def tile_dpfpattention_pa_t_kernel(tc, x, w_qk, out_0, out_1):
             rinv = small.tile([P, G], F32, name="rinv")
             nc.vector.reciprocal(rinv[:], ssums[i][:])
             nrm = work.tile([P, G, DH], F32, name="nrm")
-            m_eng = nc.vector if i in M_ON_V else nc.gpsimd
-            m_eng.tensor_tensor(
-                out=nrm[:], in0=rps[i][:], in1=rinv[:].unsqueeze(2).to_broadcast([P, G, DH]),
-                op=ALU.mult)
             nrms[i] = nrm
+            if i in M_ON_S:
+                for g in range(G):
+                    nc.scalar.activation(
+                        out=nrm[:, g, :], in_=rps[i][:, g, :], func=ACT.Copy,
+                        scale=rinv[:, g:g + 1])
+            else:
+                m_eng = nc.vector if i in M_ON_V else nc.gpsimd
+                m_eng.tensor_tensor(
+                    out=nrm[:], in0=rps[i][:], in1=rinv[:].unsqueeze(2).to_broadcast([P, G, DH]),
+                    op=ALU.mult)
+
+        def store_half(b, which):
+            t_b = BLOCK_T[b]
+            tok0 = block_tile0[b] * P
+            bb = tok0 // SEQ
+            n0 = tok0 % SEQ
+            half = (G // 2) * t_b
+            dst = (out_0, out_1)[which]
+            lo = which * half
+            nc.sync.dma_start(
+                out=dst[bb, :, n0:n0 + t_b * P, :].rearrange("h (p j) f -> p h (j f)", j=t_b),
+                in_=o_tiles[b][:, lo:lo + half, :].rearrange("p (h j) f -> p h (j f)", j=t_b),
+            )
 
         def stage_out(i):
             b = tile_block[i]
@@ -183,10 +209,19 @@ def tile_dpfpattention_pa_t_kernel(tc, x, w_qk, out_0, out_1):
             t_b = BLOCK_T[b]
             if j == 0:
                 o_tiles[b] = outp.tile([P, G * t_b, 2 * DH], F32, name="o_sb")
-            o_sb = o_tiles[b]
-            o_view = o_sb[:].rearrange("p (g j) f -> p g j f", j=t_b)
+            o_view = o_tiles[b][:].rearrange("p (g j) f -> p g j f", j=t_b)
+            acc3 = accs[i][:].rearrange("p (g i) -> p g i", g=G)
+            if i == NT - 1:
+                for lo in (0, G // 2):
+                    hi = lo + G // 2
+                    for c0, cmp in ((0, ALU.is_gt), (DH, ALU.is_lt)):
+                        nc.vector.scalar_tensor_tensor(
+                            out=o_view[:, lo:hi, j, c0:c0 + DH], in0=acc3[:, lo:hi, :], scalar=0.0,
+                            in1=nrms[i][:, lo:hi, :], op0=cmp, op1=ALU.mult)
+                    store_half(b, lo // (G // 2))
+                return
             nc.vector.scalar_tensor_tensor(
-                out=o_view[:, :, j, 0:DH], in0=accs[i], scalar=0.0, in1=nrms[i][:],
+                out=o_view[:, :, j, 0:DH], in0=acc3, scalar=0.0, in1=nrms[i][:],
                 op0=ALU.is_gt, op1=ALU.mult)
             if i in NEG_ON_G:
                 nc.gpsimd.tensor_tensor(
@@ -194,35 +229,29 @@ def tile_dpfpattention_pa_t_kernel(tc, x, w_qk, out_0, out_1):
                     op=ALU.subtract)
             else:
                 nc.vector.scalar_tensor_tensor(
-                    out=o_view[:, :, j, DH:2 * DH], in0=accs[i], scalar=0.0, in1=nrms[i][:],
+                    out=o_view[:, :, j, DH:2 * DH], in0=acc3, scalar=0.0, in1=nrms[i][:],
                     op0=ALU.is_lt, op1=ALU.mult)
 
         def store(b):
-            t_b = BLOCK_T[b]
-            tok0 = block_tile0[b] * P
-            bb = tok0 // SEQ
-            n0 = tok0 % SEQ
-            half = (G // 2) * t_b
-            for dst, lo in ((out_0, 0), (out_1, half)):
-                nc.sync.dma_start(
-                    out=dst[bb, :, n0:n0 + t_b * P, :].rearrange("h (p j) f -> p h (j f)", j=t_b),
-                    in_=o_tiles[b][:, lo:lo + half, :].rearrange("p (h j) f -> p h (j f)", j=t_b),
-                )
+            store_half(b, 0)
+            store_half(b, 1)
 
         for k in range(NT // 2):
             if COPY_STEP[k] < 0:
                 transposes(k)
-                copy_out(k)
         for q in range(len(QUANT_TILES)):
             if QUANT_STEP[q] < 0:
+                for k in range(q_start[q] // 2, (q_start[q] + QUANT_TILES[q]) // 2):
+                    copy_out(k)
                 quantise(q)
-        project(0)
+                if q == 0:
+                    project(0)
         for n in range(NT + OUT_LAG):
+            if n + 1 < NT:
+                project(n + 1)
             for k in range(NT // 2):
                 if COPY_STEP[k] == n:
                     transposes(k)
-            if n + 1 < NT:
-                project(n + 1)
             if 0 <= n - 2 < NT:
                 stage_norm(n - 2)
             if n < NT:
@@ -240,5 +269,5 @@ def tile_dpfpattention_pa_t_kernel(tc, x, w_qk, out_0, out_1):
                 if QUANT_STEP[q] == n:
                     quantise(q)
             i = n - OUT_LAG
-            if 0 <= i < NT and tile_j[i] == BLOCK_T[tile_block[i]] - 1:
+            if 0 <= i < NT - 1 and tile_j[i] == BLOCK_T[tile_block[i]] - 1:
                 store(tile_block[i])

@@ -24,7 +24,7 @@ BLOCK_T = (2, 2, 4, 4, 4, 4, 2, 2, 2, 2, 2, 1, 1)
 QUANT_TILES = (2, 2, 4, 8, 8, 8)
 COPY_STEP = (-1, -1, 0, 1, 2, 3, 4, 5, 6, 8, 10, 12, 14, 16, 18, 20)
 QUANT_STEP = (-1, -1, 1, 5, 13, 21)
-XT_ON_V = (1, 2, 3, 4, 5)
+XT_ON_V = (1, 2, 3, 4, 5, 7, 9, 11, 13, 15)
 NEG_ON_G = (2, 5, 8, 11, 14, 17, 20, 23)
 M_ON_V = ()
 M_ON_S = (30, 31)
@@ -76,6 +76,10 @@ def tile_dpfpattention_pa_t_kernel(tc, x, w_qk, out_0, out_1):
             )
             x_sbs.append(x_sb)
 
+        warm = const.tile([P, 1], F32)
+        nc.vector.memset(warm[:], 1.0)
+        nc.scalar.activation(out=warm[:], in_=warm[:], func=ACT.Abs_reciprocal_sqrt)
+
         ident = const.tile([P, P], F32)
         make_identity(nc, ident[:])
 
@@ -95,7 +99,7 @@ def tile_dpfpattention_pa_t_kernel(tc, x, w_qk, out_0, out_1):
         odds = {}
         prods = {}
         rps = {}
-        ssums = {}
+        rinvs = {}
         nrms = {}
         o_tiles = {}
 
@@ -171,12 +175,15 @@ def tile_dpfpattention_pa_t_kernel(tc, x, w_qk, out_0, out_1):
                     out=rp[:, g, :].rearrange("p (k e) -> p k e", e=2),
                     in_=prods[i][:, g, :, :].rearrange("p e k -> p k e"),
                     func=ACT.Relu, accum_out=ssum[:, g:g + 1])
+            rsq = small.tile([P, G], F32, name="rsq")
+            nc.scalar.activation(out=rsq[:], in_=ssum[:], func=ACT.Abs_reciprocal_sqrt)
+            rinv = small.tile([P, G], F32, name="rinv")
+            nc.scalar.activation(out=rinv[:], in_=rsq[:], func=ACT.Square)
             rps[i] = rp
-            ssums[i] = ssum
+            rinvs[i] = rinv
 
         def stage_norm(i):
-            rinv = small.tile([P, G], F32, name="rinv")
-            nc.vector.reciprocal(rinv[:], ssums[i][:])
+            rinv = rinvs[i]
             nrm = work.tile([P, G, DH], F32, name="nrm")
             nrms[i] = nrm
             if i in M_ON_S:

@@ -20,12 +20,12 @@ G = 8
 DH = 64
 HK = DH // 2
 OPAD = 36
-BLOCK_T = (2, 2, 4, 4, 4, 4, 2, 2, 2, 2, 2, 1, 1)
+BLOCK_T = (2, 2, 4, 4, 4, 4, 4, 2, 2, 2, 1, 1)
 QUANT_TILES = (2, 2, 4, 8, 8, 8)
 COPY_STEP = (-1, -1, 0, 1, 2, 3, 4, 5, 6, 8, 10, 12, 14, 16, 18, 20)
 QUANT_STEP = (-1, -1, 1, 5, 13, 21)
-XT_ON_V = (1, 2, 3, 4, 5, 7, 9, 11, 13, 15)
-NEG_ON_G = (2, 5, 8, 11, 14, 17, 20, 23)
+XT_ON_V = (1, 2, 3)
+NEG_ON_G = ()
 M_ON_V = ()
 M_ON_S = (30, 31)
 OUT_LAG = 4
@@ -76,10 +76,6 @@ def tile_dpfpattention_pa_t_kernel(tc, x, w_qk, out_0, out_1):
             )
             x_sbs.append(x_sb)
 
-        warm = const.tile([P, 1], F32)
-        nc.vector.memset(warm[:], 1.0)
-        nc.scalar.activation(out=warm[:], in_=warm[:], func=ACT.Abs_reciprocal_sqrt)
-
         ident = const.tile([P, P], F32)
         make_identity(nc, ident[:])
 
@@ -99,7 +95,7 @@ def tile_dpfpattention_pa_t_kernel(tc, x, w_qk, out_0, out_1):
         odds = {}
         prods = {}
         rps = {}
-        rinvs = {}
+        ssums = {}
         nrms = {}
         o_tiles = {}
 
@@ -175,15 +171,12 @@ def tile_dpfpattention_pa_t_kernel(tc, x, w_qk, out_0, out_1):
                     out=rp[:, g, :].rearrange("p (k e) -> p k e", e=2),
                     in_=prods[i][:, g, :, :].rearrange("p e k -> p k e"),
                     func=ACT.Relu, accum_out=ssum[:, g:g + 1])
-            rsq = small.tile([P, G], F32, name="rsq")
-            nc.scalar.activation(out=rsq[:], in_=ssum[:], func=ACT.Abs_reciprocal_sqrt)
-            rinv = small.tile([P, G], F32, name="rinv")
-            nc.scalar.activation(out=rinv[:], in_=rsq[:], func=ACT.Square)
             rps[i] = rp
-            rinvs[i] = rinv
+            ssums[i] = ssum
 
         def stage_norm(i):
-            rinv = rinvs[i]
+            rinv = small.tile([P, G], F32, name="rinv")
+            nc.vector.reciprocal(rinv[:], ssums[i][:])
             nrm = work.tile([P, G, DH], F32, name="nrm")
             nrms[i] = nrm
             if i in M_ON_S:

@@ -13,22 +13,24 @@ ACT = mybir.ActivationFunctionType
 
 P = 128
 D = 512
+PACK = 4
+COUPLES = D // 2
 TOKENS = 4096
 SEQ = 2048
 NT = TOKENS // P
+PAIRS = NT // 2
 G = 8
 DH = 64
-HK = DH // 2
-OPAD = 36
-BLOCK_T = (2, 2, 4, 4, 4, 4, 4, 2, 2, 2, 1, 1)
+LEAD = 4
+PADW = LEAD + DH
+
+SPAN_TILES = (2, 2, 4, 4, 4, 4, 4, 2, 2, 2, 1, 1)
 QUANT_TILES = (2, 2, 4, 8, 8, 8)
-COPY_STEP = (-1, -1, 0, 1, 2, 3, 4, 5, 6, 8, 10, 12, 14, 16, 18, 20)
-QUANT_STEP = (-1, -1, 1, 5, 13, 21)
-XT_ON_V = (1, 2, 3)
-NEG_ON_G = ()
-M_ON_V = ()
-M_ON_S = (30, 31)
-OUT_LAG = 4
+GROUPS_BEFORE_THE_PIPELINE = 2
+TILES_NORMALISED_BY_VECTOR = 2
+SUM_LAG = 1
+NORM_LAG = 2
+OUT_LAG = 3
 
 FLOPS = 2 * TOKENS * D * D
 
@@ -36,20 +38,33 @@ FLOPS = 2 * TOKENS * D * D
 def tile_dpfpattention_pa_t_kernel(tc, x, w_qk, out_0, out_1):
     nc = tc.nc
     x_flat = x.flatten_outer_dims()
-    tile_block = []
+
+    tile_span = []
     tile_j = []
-    block_tile0 = []
-    for b, t_b in enumerate(BLOCK_T):
-        block_tile0.append(len(tile_block))
-        for j in range(t_b):
-            tile_block.append(b)
+    span_tile0 = []
+    for sp, length in enumerate(SPAN_TILES):
+        span_tile0.append(len(tile_span))
+        for j in range(length):
+            tile_span.append(sp)
             tile_j.append(j)
-    assert len(tile_block) == NT
-    q_start = [sum(QUANT_TILES[:q]) for q in range(len(QUANT_TILES))]
+    assert len(tile_span) == NT
+    group_tile0 = [sum(QUANT_TILES[:q]) for q in range(len(QUANT_TILES))]
     assert sum(QUANT_TILES) == NT
-    tile_q = []
-    for q, n_q in enumerate(QUANT_TILES):
-        tile_q.extend([q] * n_q)
+    tile_group = []
+    for q, tiles in enumerate(QUANT_TILES):
+        tile_group.extend([q] * tiles)
+
+    copy_step = []
+    quant_step = []
+    for q, tiles in enumerate(QUANT_TILES):
+        if q < GROUPS_BEFORE_THE_PIPELINE:
+            copy_step.extend([-1] * (tiles // 2))
+            quant_step.append(-1)
+        else:
+            distance = QUANT_TILES[q - 1] // (tiles // 2)
+            for place in range(tiles // 2):
+                copy_step.append(group_tile0[q - 1] - 2 + place * distance)
+            quant_step.append(group_tile0[q] - 3)
 
     with ExitStack() as ctx:
         const = ctx.enter_context(tc.tile_pool(name="const", bufs=1))
@@ -61,28 +76,28 @@ def tile_dpfpattention_pa_t_kernel(tc, x, w_qk, out_0, out_1):
         ps_a = ctx.enter_context(tc.psum_pool(name="ps_a", bufs=6))
         ctx.enter_context(tc.manual_schedule())
 
-        w_sb = const.tile([P, 4, D], BF16)
+        w_sb = const.tile([P, PACK, D], BF16)
         nc.sync.dma_start(
-            out=w_sb[:].rearrange("q (u e) c -> q u (e c)", u=2),
-            in_=w_qk.rearrange("(u q e) c -> q u (e c)", u=2, e=2),
+            out=w_sb[:].rearrange("p (s e) c -> p s (e c)", s=2),
+            in_=w_qk.rearrange("(s p e) c -> p s (e c)", s=2, e=2),
         )
         x_sbs = []
-        for b, t_b in enumerate(BLOCK_T):
-            x_sb = const.tile([P, t_b * D], BF16, name="x_sb%d" % b)
-            r0 = block_tile0[b] * P
+        for sp, length in enumerate(SPAN_TILES):
+            x_sb = const.tile([P, length * D], BF16, name="x_sb%d" % sp)
+            token0 = span_tile0[sp] * P
             nc.sync.dma_start(
                 out=x_sb[:],
-                in_=x_flat[r0:r0 + t_b * P, :].rearrange("(p j) k -> p (j k)", j=t_b),
+                in_=x_flat[token0:token0 + length * P, :].rearrange("(p j) k -> p (j k)", j=length),
             )
             x_sbs.append(x_sb)
 
         ident = const.tile([P, P], F32)
         make_identity(nc, ident[:])
 
-        w_grp = const.tile([P, D * 4], BF16, align_bytes=64)
+        w_grp = const.tile([P, D * PACK], BF16, align_bytes=64)
         nc.vector.tensor_copy(
-            out=w_grp[:].rearrange("p (c i t) -> p c t i", i=4, t=4),
-            in_=w_sb[:].rearrange("p t (c i) -> p c t i", i=4),
+            out=w_grp[:].rearrange("p (c a t) -> p c t a", a=4, t=PACK),
+            in_=w_sb[:].rearrange("p t (c a) -> p c t a", a=4),
         )
         w_codes = const.tile([P, D], U32, align_bytes=64)
         w_scales = const.tile([P, D], U8, align_bytes=64)
@@ -92,48 +107,49 @@ def tile_dpfpattention_pa_t_kernel(tc, x, w_qk, out_0, out_1):
         x_grps = {}
         codes = {}
         accs = {}
-        odds = {}
+        u_pads = {}
         prods = {}
         rps = {}
         ssums = {}
         nrms = {}
         o_tiles = {}
 
-        def transposes(k):
+        def transposes(pair):
             xt = ps_t.tile([P, 2, 2, P], F32, name="xt")
-            for jj in range(2):
-                i = 2 * k + jj
-                xw = x_sbs[tile_block[i]][:].bitcast(F32)
-                for u in range(2):
-                    c0 = tile_j[i] * 256 + u * P
-                    nc.tensor.transpose(xt[:, jj, u, :], xw[:, c0:c0 + P], ident[:])
-            xts[k] = xt
+            for d in range(2):
+                ti = 2 * pair + d
+                couples = x_sbs[tile_span[ti]][:].bitcast(F32)
+                for s in range(2):
+                    c0 = tile_j[ti] * COUPLES + s * P
+                    nc.tensor.transpose(xt[:, d, s, :], couples[:, c0:c0 + P], ident[:])
+            xts[pair] = xt
 
-        def copy_out(k):
-            q = tile_q[2 * k]
-            if 2 * k == q_start[q]:
+        def copy_out(pair):
+            q = tile_group[2 * pair]
+            if 2 * pair == group_tile0[q]:
                 x_grps[q] = xq.tile([P, QUANT_TILES[q] * D], BF16, align_bytes=64, name="x_grp")
-            h = k - q_start[q] // 2
-            dst = x_grps[q][:].bitcast(F32)[:, h * 512:(h + 1) * 512].rearrange(
-                "p (j r u) -> p j r u", j=2, u=2)
-            src = xts[k][:].rearrange("p j u r -> p j r u")
-            if k in XT_ON_V:
+            place = pair - group_tile0[q] // 2
+            c0 = place * 2 * COUPLES
+            dst = x_grps[q][:].bitcast(F32)[:, c0:c0 + 2 * COUPLES].rearrange(
+                "p (d r s) -> p d r s", d=2, s=2)
+            src = xts[pair][:].rearrange("p d s r -> p d r s")
+            if pair > 0 and copy_step[pair] < OUT_LAG:
                 nc.vector.tensor_copy(out=dst, in_=src)
             else:
                 nc.scalar.copy(out=dst, in_=src)
 
         def quantise(q):
-            n_q = QUANT_TILES[q]
-            x_codes = const.tile([P, n_q * P], U32, align_bytes=64, name="x_codes%d" % q)
-            x_scales = const.tile([P, n_q * P], U8, align_bytes=64, name="x_scales%d" % q)
+            width = QUANT_TILES[q] * P
+            x_codes = const.tile([P, width], U32, align_bytes=64, name="x_codes%d" % q)
+            x_scales = const.tile([P, width], U8, align_bytes=64, name="x_scales%d" % q)
             nc.vector.quantize_mx(
                 out=x_codes[:].bitcast(FP8X4), scales=x_scales[:], in_=x_grps[q][:])
             codes[q] = (x_codes, x_scales)
 
-        def project(i):
-            q = tile_q[i]
+        def project(ti):
+            q = tile_group[ti]
             x_codes, x_scales = codes[q]
-            c0 = (i - q_start[q]) * P
+            c0 = (ti - group_tile0[q]) * P
             acc = ps_a.tile([P, D], F32, name="acc")
             nc.tensor.matmul_mx(
                 out=acc[:],
@@ -144,130 +160,101 @@ def tile_dpfpattention_pa_t_kernel(tc, x, w_qk, out_0, out_1):
                 start=True,
                 stop=True,
             )
-            accs[i] = acc
+            accs[ti] = acc[:].rearrange("p (g i) -> p g i", g=G)
 
-        def stage_up(i):
-            acc4 = accs[i][:].rearrange("p (g k e) -> p g k e", g=G, e=2)
-            odd = work.tile([P, G, OPAD], F32, name="odd")
-            nc.scalar.copy(out=odd[:, :, 4:OPAD], in_=acc4[:, :, :, 1])
+        def copy_u(ti):
+            u_pad = work.tile([P, G, PADW], F32, name="u_pad")
+            nc.scalar.copy(out=u_pad[:, :, LEAD:PADW], in_=accs[ti])
             nc.scalar.activation(
-                out=odd[:, :, 3:4], in_=acc4[:, :, HK - 1:HK, 1], func=ACT.Copy, scale=-1.0)
-            odds[i] = odd
+                out=u_pad[:, :, LEAD - 1:LEAD], in_=accs[ti][:, :, DH - 1:DH], func=ACT.Copy,
+                scale=-1.0)
+            u_pads[ti] = u_pad
 
-        def stage_p(i):
-            even = accs[i][:].rearrange("p (g k e) -> p g k e", g=G, e=2)[:, :, :, 0]
-            prod = work.tile([P, G, 2, HK], F32, name="prod")
-            for e in range(2):
-                nc.vector.tensor_tensor(
-                    out=prod[:, :, e, :], in0=even, in1=odds[i][:, :, 3 + e:3 + e + HK],
-                    op=ALU.mult)
-            prods[i] = prod
+        def multiply(ti):
+            prod = work.tile([P, G, DH], F32, name="prod")
+            nc.vector.tensor_tensor(
+                out=prod[:], in0=accs[ti], in1=u_pads[ti][:, :, LEAD - 1:PADW - 1], op=ALU.mult)
+            prods[ti] = prod
 
-        def stage_sum(i):
+        def relu_and_sum(ti):
             rp = work.tile([P, G, DH], F32, name="rp")
             ssum = small.tile([P, G], F32, name="ssum")
             for g in range(G):
                 nc.scalar.activation(
-                    out=rp[:, g, :].rearrange("p (k e) -> p k e", e=2),
-                    in_=prods[i][:, g, :, :].rearrange("p e k -> p k e"),
-                    func=ACT.Relu, accum_out=ssum[:, g:g + 1])
-            rps[i] = rp
-            ssums[i] = ssum
+                    out=rp[:, g, :], in_=prods[ti][:, g, :], func=ACT.Relu,
+                    accum_out=ssum[:, g:g + 1])
+            rps[ti] = rp
+            ssums[ti] = ssum
 
-        def stage_norm(i):
+        def normalise(ti):
             rinv = small.tile([P, G], F32, name="rinv")
-            nc.vector.reciprocal(rinv[:], ssums[i][:])
+            nc.vector.reciprocal(rinv[:], ssums[ti][:])
             nrm = work.tile([P, G, DH], F32, name="nrm")
-            nrms[i] = nrm
-            if i in M_ON_S:
-                for g in range(G):
-                    nc.scalar.activation(
-                        out=nrm[:, g, :], in_=rps[i][:, g, :], func=ACT.Copy,
-                        scale=rinv[:, g:g + 1])
-            else:
-                m_eng = nc.vector if i in M_ON_V else nc.gpsimd
-                m_eng.tensor_tensor(
-                    out=nrm[:], in0=rps[i][:], in1=rinv[:].unsqueeze(2).to_broadcast([P, G, DH]),
-                    op=ALU.mult)
+            engine = nc.vector if ti >= NT - TILES_NORMALISED_BY_VECTOR else nc.gpsimd
+            engine.tensor_tensor(
+                out=nrm[:], in0=rps[ti][:], in1=rinv[:].unsqueeze(2).to_broadcast([P, G, DH]),
+                op=ALU.mult)
+            nrms[ti] = nrm
 
-        def store_half(b, which):
-            t_b = BLOCK_T[b]
-            tok0 = block_tile0[b] * P
-            bb = tok0 // SEQ
-            n0 = tok0 % SEQ
-            half = (G // 2) * t_b
-            dst = (out_0, out_1)[which]
-            lo = which * half
-            nc.sync.dma_start(
-                out=dst[bb, :, n0:n0 + t_b * P, :].rearrange("h (p j) f -> p h (j f)", j=t_b),
-                in_=o_tiles[b][:, lo:lo + half, :].rearrange("p (h j) f -> p h (j f)", j=t_b),
-            )
-
-        def stage_out(i):
-            b = tile_block[i]
-            j = tile_j[i]
-            t_b = BLOCK_T[b]
+        def write_halves(ti):
+            sp = tile_span[ti]
+            j = tile_j[ti]
+            length = SPAN_TILES[sp]
             if j == 0:
-                o_tiles[b] = outp.tile([P, G * t_b, 2 * DH], F32, name="o_sb")
-            o_view = o_tiles[b][:].rearrange("p (g j) f -> p g j f", j=t_b)
-            acc3 = accs[i][:].rearrange("p (g i) -> p g i", g=G)
-            if i == NT - 1:
-                for lo in (0, G // 2):
-                    hi = lo + G // 2
-                    for c0, cmp in ((0, ALU.is_gt), (DH, ALU.is_lt)):
-                        nc.vector.scalar_tensor_tensor(
-                            out=o_view[:, lo:hi, j, c0:c0 + DH], in0=acc3[:, lo:hi, :], scalar=0.0,
-                            in1=nrms[i][:, lo:hi, :], op0=cmp, op1=ALU.mult)
-                    store_half(b, lo // (G // 2))
-                return
+                o_tiles[sp] = outp.tile([P, G * length, 2 * DH], F32, name="o_sb")
+            o_view = o_tiles[sp][:].rearrange("p (g j) f -> p g j f", j=length)
             nc.vector.scalar_tensor_tensor(
-                out=o_view[:, :, j, 0:DH], in0=acc3, scalar=0.0, in1=nrms[i][:],
+                out=o_view[:, :, j, 0:DH], in0=accs[ti], scalar=0.0, in1=nrms[ti][:],
                 op0=ALU.is_gt, op1=ALU.mult)
-            if i in NEG_ON_G:
-                nc.gpsimd.tensor_tensor(
-                    out=o_view[:, :, j, DH:2 * DH], in0=nrms[i][:], in1=o_view[:, :, j, 0:DH],
-                    op=ALU.subtract)
-            else:
-                nc.vector.scalar_tensor_tensor(
-                    out=o_view[:, :, j, DH:2 * DH], in0=acc3, scalar=0.0, in1=nrms[i][:],
-                    op0=ALU.is_lt, op1=ALU.mult)
+            nc.vector.scalar_tensor_tensor(
+                out=o_view[:, :, j, DH:2 * DH], in0=accs[ti], scalar=0.0, in1=nrms[ti][:],
+                op0=ALU.is_lt, op1=ALU.mult)
 
-        def store(b):
-            store_half(b, 0)
-            store_half(b, 1)
+        def store(sp):
+            length = SPAN_TILES[sp]
+            token0 = span_tile0[sp] * P
+            batch = token0 // SEQ
+            first = token0 % SEQ
+            rows = (G // 2) * length
+            for dst, lo in ((out_0, 0), (out_1, rows)):
+                nc.sync.dma_start(
+                    out=dst[batch, :, first:first + length * P, :].rearrange(
+                        "g (p j) f -> p g (j f)", j=length),
+                    in_=o_tiles[sp][:, lo:lo + rows, :].rearrange(
+                        "p (g j) f -> p g (j f)", j=length),
+                )
 
-        for k in range(NT // 2):
-            if COPY_STEP[k] < 0:
-                transposes(k)
+        for pair in range(PAIRS):
+            if copy_step[pair] < 0:
+                transposes(pair)
+                copy_out(pair)
         for q in range(len(QUANT_TILES)):
-            if QUANT_STEP[q] < 0:
-                for k in range(q_start[q] // 2, (q_start[q] + QUANT_TILES[q]) // 2):
-                    copy_out(k)
+            if quant_step[q] < 0:
                 quantise(q)
-                if q == 0:
-                    project(0)
+        project(0)
+
         for n in range(NT + OUT_LAG):
+            for pair in range(PAIRS):
+                if copy_step[pair] == n:
+                    transposes(pair)
             if n + 1 < NT:
                 project(n + 1)
-            for k in range(NT // 2):
-                if COPY_STEP[k] == n:
-                    transposes(k)
-            if 0 <= n - 2 < NT:
-                stage_norm(n - 2)
+            if 0 <= n - NORM_LAG < NT:
+                normalise(n - NORM_LAG)
             if n < NT:
-                stage_up(n)
+                copy_u(n)
             if 0 <= n - OUT_LAG < NT:
-                stage_out(n - OUT_LAG)
-            if 0 <= n - 1 < NT:
-                stage_sum(n - 1)
+                write_halves(n - OUT_LAG)
+            if 0 <= n - SUM_LAG < NT:
+                relu_and_sum(n - SUM_LAG)
             if n < NT:
-                stage_p(n)
-            for k in range(NT // 2):
-                if COPY_STEP[k] == n:
-                    copy_out(k)
+                multiply(n)
+            for pair in range(PAIRS):
+                if copy_step[pair] == n:
+                    copy_out(pair)
             for q in range(len(QUANT_TILES)):
-                if QUANT_STEP[q] == n:
+                if quant_step[q] == n:
                     quantise(q)
-            i = n - OUT_LAG
-            if 0 <= i < NT - 1 and tile_j[i] == BLOCK_T[tile_block[i]] - 1:
-                store(tile_block[i])
+            done = n - OUT_LAG
+            if 0 <= done < NT and tile_j[done] == SPAN_TILES[tile_span[done]] - 1:
+                store(tile_span[done])

from contextlib import ExitStack

import concourse.mybir as mybir
from concourse.masks import make_identity

F32 = mybir.dt.float32
BF16 = mybir.dt.bfloat16
U32 = mybir.dt.uint32
U8 = mybir.dt.uint8
FP8X4 = mybir.dt.float8_e4m3fn_x4
ALU = mybir.AluOpType
ACT = mybir.ActivationFunctionType

P = 128
D = 512
PACK = 4
COUPLES = D // 2
TOKENS = 4096
SEQ = 2048
NT = TOKENS // P
PAIRS = NT // 2
G = 8
DH = 64
LEAD = 4
PADW = LEAD + DH

SPAN_TILES = (2, 2, 4, 4, 4, 4, 4, 2, 2, 2, 1, 1)
QUANT_TILES = (2, 2, 4, 8, 8, 8)
GROUPS_BEFORE_THE_PIPELINE = 2
TILES_NORMALISED_BY_VECTOR = 2
SUM_LAG = 1
NORM_LAG = 2
OUT_LAG = 3

FLOPS = 2 * TOKENS * D * D


def tile_dpfpattention_pa_t_kernel(tc, x, w_qk, out_0, out_1):
    nc = tc.nc
    x_flat = x.flatten_outer_dims()

    tile_span = []
    tile_j = []
    span_tile0 = []
    for sp, length in enumerate(SPAN_TILES):
        span_tile0.append(len(tile_span))
        for j in range(length):
            tile_span.append(sp)
            tile_j.append(j)
    assert len(tile_span) == NT
    group_tile0 = [sum(QUANT_TILES[:q]) for q in range(len(QUANT_TILES))]
    assert sum(QUANT_TILES) == NT
    tile_group = []
    for q, tiles in enumerate(QUANT_TILES):
        tile_group.extend([q] * tiles)

    copy_step = []
    quant_step = []
    for q, tiles in enumerate(QUANT_TILES):
        if q < GROUPS_BEFORE_THE_PIPELINE:
            copy_step.extend([-1] * (tiles // 2))
            quant_step.append(-1)
        else:
            distance = QUANT_TILES[q - 1] // (tiles // 2)
            for place in range(tiles // 2):
                copy_step.append(group_tile0[q - 1] - 2 + place * distance)
            quant_step.append(group_tile0[q] - 3)

    with ExitStack() as ctx:
        const = ctx.enter_context(tc.tile_pool(name="const", bufs=1))
        xq = ctx.enter_context(tc.tile_pool(name="xq", bufs=2))
        work = ctx.enter_context(tc.tile_pool(name="work", bufs=4))
        small = ctx.enter_context(tc.tile_pool(name="small", bufs=8))
        outp = ctx.enter_context(tc.tile_pool(name="outp", bufs=5))
        ps_t = ctx.enter_context(tc.psum_pool(name="ps_t", bufs=2))
        ps_a = ctx.enter_context(tc.psum_pool(name="ps_a", bufs=6))
        ctx.enter_context(tc.manual_schedule())

        w_sb = const.tile([P, PACK, D], BF16)
        nc.sync.dma_start(
            out=w_sb[:].rearrange("p (s e) c -> p s (e c)", s=2),
            in_=w_qk.rearrange("(s p e) c -> p s (e c)", s=2, e=2),
        )
        x_sbs = []
        for sp, length in enumerate(SPAN_TILES):
            x_sb = const.tile([P, length * D], BF16, name="x_sb%d" % sp)
            token0 = span_tile0[sp] * P
            nc.sync.dma_start(
                out=x_sb[:],
                in_=x_flat[token0:token0 + length * P, :].rearrange("(p j) k -> p (j k)", j=length),
            )
            x_sbs.append(x_sb)

        ident = const.tile([P, P], F32)
        make_identity(nc, ident[:])

        w_grp = const.tile([P, D * PACK], BF16, align_bytes=64)
        nc.vector.tensor_copy(
            out=w_grp[:].rearrange("p (c a t) -> p c t a", a=4, t=PACK),
            in_=w_sb[:].rearrange("p t (c a) -> p c t a", a=4),
        )
        w_codes = const.tile([P, D], U32, align_bytes=64)
        w_scales = const.tile([P, D], U8, align_bytes=64)
        nc.vector.quantize_mx(out=w_codes[:].bitcast(FP8X4), scales=w_scales[:], in_=w_grp[:])

        xts = {}
        x_grps = {}
        codes = {}
        accs = {}
        u_pads = {}
        prods = {}
        rps = {}
        ssums = {}
        nrms = {}
        o_tiles = {}

        def transposes(pair):
            xt = ps_t.tile([P, 2, 2, P], F32, name="xt")
            for d in range(2):
                ti = 2 * pair + d
                couples = x_sbs[tile_span[ti]][:].bitcast(F32)
                for s in range(2):
                    c0 = tile_j[ti] * COUPLES + s * P
                    nc.tensor.transpose(xt[:, d, s, :], couples[:, c0:c0 + P], ident[:])
            xts[pair] = xt

        def copy_out(pair):
            q = tile_group[2 * pair]
            if 2 * pair == group_tile0[q]:
                x_grps[q] = xq.tile([P, QUANT_TILES[q] * D], BF16, align_bytes=64, name="x_grp")
            place = pair - group_tile0[q] // 2
            c0 = place * 2 * COUPLES
            dst = x_grps[q][:].bitcast(F32)[:, c0:c0 + 2 * COUPLES].rearrange(
                "p (d r s) -> p d r s", d=2, s=2)
            src = xts[pair][:].rearrange("p d s r -> p d r s")
            if pair > 0 and copy_step[pair] < OUT_LAG:
                nc.vector.tensor_copy(out=dst, in_=src)
            else:
                nc.scalar.copy(out=dst, in_=src)

        def quantise(q):
            width = QUANT_TILES[q] * P
            x_codes = const.tile([P, width], U32, align_bytes=64, name="x_codes%d" % q)
            x_scales = const.tile([P, width], U8, align_bytes=64, name="x_scales%d" % q)
            nc.vector.quantize_mx(
                out=x_codes[:].bitcast(FP8X4), scales=x_scales[:], in_=x_grps[q][:])
            codes[q] = (x_codes, x_scales)

        def project(ti):
            q = tile_group[ti]
            x_codes, x_scales = codes[q]
            c0 = (ti - group_tile0[q]) * P
            acc = ps_a.tile([P, D], F32, name="acc")
            nc.tensor.matmul_mx(
                out=acc[:],
                lhsT=x_codes[:, c0:c0 + P].bitcast(FP8X4),
                lhsT_scale=x_scales[:, c0:c0 + P],
                rhs=w_codes[:].bitcast(FP8X4),
                rhs_scale=w_scales[:],
                start=True,
                stop=True,
            )
            accs[ti] = acc[:].rearrange("p (g i) -> p g i", g=G)

        def copy_u(ti):
            u_pad = work.tile([P, G, PADW], F32, name="u_pad")
            nc.scalar.copy(out=u_pad[:, :, LEAD:PADW], in_=accs[ti])
            nc.scalar.activation(
                out=u_pad[:, :, LEAD - 1:LEAD], in_=accs[ti][:, :, DH - 1:DH], func=ACT.Copy,
                scale=-1.0)
            u_pads[ti] = u_pad

        def multiply(ti):
            prod = work.tile([P, G, DH], F32, name="prod")
            nc.vector.tensor_tensor(
                out=prod[:], in0=accs[ti], in1=u_pads[ti][:, :, LEAD - 1:PADW - 1], op=ALU.mult)
            prods[ti] = prod

        def relu_and_sum(ti):
            rp = work.tile([P, G, DH], F32, name="rp")
            ssum = small.tile([P, G], F32, name="ssum")
            for g in range(G):
                nc.scalar.activation(
                    out=rp[:, g, :], in_=prods[ti][:, g, :], func=ACT.Relu,
                    accum_out=ssum[:, g:g + 1])
            rps[ti] = rp
            ssums[ti] = ssum

        def normalise(ti):
            rinv = small.tile([P, G], F32, name="rinv")
            nc.vector.reciprocal(rinv[:], ssums[ti][:])
            nrm = work.tile([P, G, DH], F32, name="nrm")
            engine = nc.vector if ti >= NT - TILES_NORMALISED_BY_VECTOR else nc.gpsimd
            engine.tensor_tensor(
                out=nrm[:], in0=rps[ti][:], in1=rinv[:].unsqueeze(2).to_broadcast([P, G, DH]),
                op=ALU.mult)
            nrms[ti] = nrm

        def write_halves(ti):
            sp = tile_span[ti]
            j = tile_j[ti]
            length = SPAN_TILES[sp]
            if j == 0:
                o_tiles[sp] = outp.tile([P, G * length, 2 * DH], F32, name="o_sb")
            o_view = o_tiles[sp][:].rearrange("p (g j) f -> p g j f", j=length)
            nc.vector.scalar_tensor_tensor(
                out=o_view[:, :, j, 0:DH], in0=accs[ti], scalar=0.0, in1=nrms[ti][:],
                op0=ALU.is_gt, op1=ALU.mult)
            nc.vector.scalar_tensor_tensor(
                out=o_view[:, :, j, DH:2 * DH], in0=accs[ti], scalar=0.0, in1=nrms[ti][:],
                op0=ALU.is_lt, op1=ALU.mult)

        def store(sp):
            length = SPAN_TILES[sp]
            token0 = span_tile0[sp] * P
            batch = token0 // SEQ
            first = token0 % SEQ
            rows = (G // 2) * length
            for dst, lo in ((out_0, 0), (out_1, rows)):
                nc.sync.dma_start(
                    out=dst[batch, :, first:first + length * P, :].rearrange(
                        "g (p j) f -> p g (j f)", j=length),
                    in_=o_tiles[sp][:, lo:lo + rows, :].rearrange(
                        "p (g j) f -> p g (j f)", j=length),
                )

        for pair in range(PAIRS):
            if copy_step[pair] < 0:
                transposes(pair)
                copy_out(pair)
        for q in range(len(QUANT_TILES)):
            if quant_step[q] < 0:
                quantise(q)
        project(0)

        for n in range(NT + OUT_LAG):
            for pair in range(PAIRS):
                if copy_step[pair] == n:
                    transposes(pair)
            if n + 1 < NT:
                project(n + 1)
            if 0 <= n - NORM_LAG < NT:
                normalise(n - NORM_LAG)
            if n < NT:
                copy_u(n)
            if 0 <= n - OUT_LAG < NT:
                write_halves(n - OUT_LAG)
            if 0 <= n - SUM_LAG < NT:
                relu_and_sum(n - SUM_LAG)
            if n < NT:
                multiply(n)
            for pair in range(PAIRS):
                if copy_step[pair] == n:
                    copy_out(pair)
            for q in range(len(QUANT_TILES)):
                if quant_step[q] == n:
                    quantise(q)
            done = n - OUT_LAG
            if 0 <= done < NT and tile_j[done] == SPAN_TILES[tile_span[done]] - 1:
                store(tile_span[done])
